import numpy as np
import ml_dtypes


def mxq(x, axis, fmt="e4m3"):
    dtype, down = {"e4m3": (ml_dtypes.float8_e4m3fn, 7), "e5m2": (ml_dtypes.float8_e5m2, 14)}[fmt]
    v = np.moveaxis(np.asarray(x, np.float32).astype(ml_dtypes.bfloat16).astype(np.float64), axis, -1)
    blocks = v.reshape(v.shape[:-1] + (-1, 32))
    amax = np.abs(blocks).max(-1, keepdims=True)
    byte = np.maximum(np.where(amax > 0, np.frexp(amax)[1] - 1 + 127, 0) - down, 1)
    scale = np.exp2(byte - 127.0)
    codes = (blocks / scale).astype(np.float32).astype(dtype).astype(np.float64)
    return np.moveaxis((codes * scale).reshape(v.shape), -1, axis)


WIDE = False


def mx_kscale(k):
    if not WIDE:
        return np.ones(k)
    levels = np.array([10, -10, 5, -5, 0])
    a = np.random.permutation(np.resize(levels, k // 512 * 4)).reshape(k // 512, 4)
    idx = np.arange(k)
    return np.exp2(a[idx // 512, idx % 128 // 32])


BF16 = ml_dtypes.bfloat16


def bf(x):
    return np.asarray(x, np.float32).astype(BF16)


def f64(x):
    return np.asarray(x).astype(np.float64)


E2M1 = np.array([0.0, 0.5, 1.0, 1.5, 2.0, 3.0, 4.0, 6.0, -0.0, -0.5, -1.0, -1.5, -2.0, -3.0, -4.0, -6.0])


def pack_weight(w, fmt):
    k, n = w.shape
    w = f64(bf(w)).reshape(k // 32, 32, n)
    amax = np.abs(w).max(1)
    if fmt == "e4m3":
        byte = np.frexp(amax)[1] - 1 + 127 - 7
    else:
        mant, ex = np.frexp(amax / 6.0)
        byte = np.where(mant > 0.5, ex, ex - 1) + 127
    byte = np.clip(np.where(amax > 0, byte, 1), 1, 254)
    scaled = (w * np.exp2(127.0 - byte)[:, None, :]).reshape(k, n).astype(np.float32)
    by_word = np.ascontiguousarray(scaled.reshape(k // 512, 128, 4, n).transpose(0, 1, 3, 2))
    if fmt == "e4m3":
        words = by_word.astype(ml_dtypes.float8_e4m3fn).view(np.uint8)
    else:
        c = by_word.astype(ml_dtypes.float4_e2m1fn).view(np.uint8) & 0xF
        words = c[..., 0::2] | (c[..., 1::2] << 4)
    return np.ascontiguousarray(words), np.ascontiguousarray(byte.astype(np.uint8).reshape(k // 512, 16, n))


def unpack_weight(words, scales, fmt):
    g, p, n, _ = words.shape
    if fmt == "e4m3":
        vals = np.ascontiguousarray(words).view(ml_dtypes.float8_e4m3fn).astype(np.float64)
    else:
        nib = np.empty((g, p, n, 4), np.uint8)
        nib[..., 0::2] = words & 0xF
        nib[..., 1::2] = words >> 4
        vals = E2M1[nib]
    vals = vals * np.repeat(np.exp2(scales.astype(np.float64) - 127.0), 8, axis=1)[..., None]
    return vals.transpose(0, 1, 3, 2).reshape(g * 512, n)

def pack4(w):
    words, scales = pack_weight(w, "e2m1")
    return words.reshape(words.shape[0], 128, -1), scales


def unpack4(words, scales):
    return unpack_weight(words.reshape(words.shape[0], 128, -1, 2), scales, "e2m1")


B, S, D, E, HD = 4, 1024, 512, 1024, 64
ROPE_BASE = 10000.0


def rope_tables():
    inv_freq = 1.0 / ROPE_BASE ** (np.arange(0, E, 2) / E)
    ang = np.repeat(np.arange(S)[:, None] * inv_freq[None, :], 2, axis=-1)
    return np.cos(ang), np.sin(ang)


def rotate_half(v):
    h = v.shape[-1] // 2
    return np.concatenate([-v[..., h:], v[..., :h]], axis=-1)


def setup_inputs():
    s = mx_kscale(D)
    x = bf(np.random.standard_normal((B, S, D)) * s)
    Wq_words, Wq_scales = pack4(np.random.standard_normal((D, E)) * 0.5 / np.sqrt(D) / s[:, None])
    bq = bf(np.random.standard_normal(E) * 0.1)
    Wk_words, Wk_scales = pack4(np.random.standard_normal((D, E)) * 0.5 / np.sqrt(D) / s[:, None])
    bk = bf(np.random.standard_normal(E) * 0.1)
    return {"x": x,
            "Wq_words": Wq_words,
            "Wq_scales": Wq_scales,
            "bq": bq,
            "Wk_words": Wk_words,
            "Wk_scales": Wk_scales,
            "bk": bk}


def reference(x, Wq_words, Wq_scales, bq, Wk_words, Wk_scales, bk):
    xq = mxq(f64(x), 2, "e4m3")
    q = (xq @ unpack4(Wq_words, Wq_scales)) + f64(bq)
    k = (xq @ unpack4(Wk_words, Wk_scales)) + f64(bk)
    cos, sin = rope_tables()
    qr = q * cos + rotate_half(q) * sin
    kr = k * cos + rotate_half(k) * sin
    return qr, kr

@@ -1,0 +1,334 @@
+import math
+from contextlib import ExitStack
+
+import concourse.mybir as mybir
+from concourse.masks import make_identity
+
+F32 = mybir.dt.float32
+BF16 = mybir.dt.bfloat16
+I32 = mybir.dt.int32
+U32 = mybir.dt.uint32
+U8 = mybir.dt.uint8
+FP8X4 = mybir.dt.float8_e4m3fn_x4
+FP4X4 = mybir.dt.float4_e2m1fn_x4
+ALU = mybir.AluOpType
+ACT = mybir.ActivationFunctionType
+
+P = 128
+BATCH, SEQ, DIM, FEAT = 4, 1024, 512, 1024
+ROPE_BASE = 10000.0
+TOKENS = 512
+BLOCKS = TOKENS // P
+SPANS = SEQ // TOKENS
+TILES = FEAT // P
+PAIRS = TILES // 2
+WORDS = DIM // 2
+SUMMED = 1
+JOINED = 2
+
+FLOPS = 2 * BATCH * SEQ * DIM * 2 * FEAT
+
+
+def tile_ropemultiheadattention_pa_t_kernel(
+    tc, x, Wq_words, Wq_scales, bq, Wk_words, Wk_scales, bk, out_0, out_1
+):
+    nc = tc.nc
+    outs = (out_0, out_1)
+
+    with ExitStack() as pools:
+        const = pools.enter_context(tc.tile_pool(name="const", bufs=1))
+        angle = pools.enter_context(tc.tile_pool(name="angle", bufs=2))
+        x_in = pools.enter_context(tc.tile_pool(name="x_in", bufs=3))
+        x_mx = pools.enter_context(tc.tile_pool(name="x_mx", bufs=2))
+        rotated = pools.enter_context(tc.tile_pool(name="rotated", bufs=4))
+        lifted = pools.enter_context(tc.tile_pool(name="lifted", bufs=2))
+        staging = pools.enter_context(tc.tile_pool(name="staging", bufs=4))
+        keep_ps = pools.enter_context(tc.psum_pool(name="keep_ps", bufs=1))
+        turn_ps = pools.enter_context(tc.psum_pool(name="turn_ps", bufs=7))
+
+        groups = [(batch, span) for span in range(SPANS) for batch in range(BATCH)]
+
+        def load_x(g):
+            batch, span = groups[g]
+            rows = x[batch, span * TOKENS : (span + 1) * TOKENS, :]
+            x_rows = x_in.tile([P, BLOCKS, DIM], BF16)
+            nc.sync.dma_start(out=x_rows[:], in_=rows.rearrange("(n p) k -> p n k", p=P))
+            return x_rows
+
+        loaded = {0: load_x(0)}
+        bias_rows = const.tile([P, P], BF16)
+        nc.vector.memset(bias_rows[:], 0.0)
+        nc.sync.dma_start(out=bias_rows[0:TILES, :], in_=bq.rearrange("(t p) -> t p", p=P))
+        nc.sync.dma_start(out=bias_rows[TILES : 2 * TILES, :], in_=bk.rearrange("(t p) -> t p", p=P))
+        w_words = const.tile([P, 2, 2 * FEAT], U8, align_bytes=64)
+        w_scales = const.tile([P, 2, FEAT], U8, align_bytes=64)
+        nc.vector.memset(w_scales[:].bitcast(I32), 0)
+        for proj, (words, scales) in enumerate(((Wq_words, Wq_scales), (Wk_words, Wk_scales))):
+            nc.sync.dma_start(out=w_words[:, proj, :].bitcast(I32), in_=words[0].bitcast(I32))
+            for quad in range(4):
+                nc.sync.dma_start(
+                    out=w_scales[32 * quad : 32 * quad + 4, proj, :].bitcast(I32),
+                    in_=scales[0, 4 * quad : 4 * quad + 4, :].bitcast(I32),
+                )
+        loaded[1] = load_x(1)
+
+        ident = const.tile([P, P], F32)
+        make_identity(nc, ident[:])
+
+        ratio = ROPE_BASE ** (-2.0 / FEAT)
+        ratio_row = const.tile([P, P], F32)
+        nc.vector.memset(ratio_row[:, 0:2], 1.0)
+        width = 2
+        while width < P:
+            nc.vector.tensor_scalar_mul(
+                out=ratio_row[:, width : 2 * width],
+                in0=ratio_row[:, 0:width],
+                scalar1=ratio ** (width // 2),
+            )
+            width *= 2
+
+        turned = keep_ps.tile([P, 2, P], F32)
+        nc.tensor.transpose(turned[:, 1, :], ratio_row[:], ident[:])
+
+        position = const.tile([P, SEQ], F32)
+        nc.gpsimd.iota(
+            position[:], pattern=[[1, SEQ]], base=0, channel_multiplier=0, allow_small_or_imprecise_dtypes=True
+        )
+
+        quarter = const.tile([P, 1], F32)
+        nc.vector.memset(quarter[:], 0.25)
+        quarter_turn = const.tile([P, 1], F32)
+        nc.vector.tensor_scalar_mul(out=quarter_turn[:], in0=quarter[:], scalar1=2.0 * math.pi)
+
+        turns = const.tile([P, PAIRS, 2], F32)
+        for h in range(PAIRS):
+            for j in range(2):
+                first = ratio ** ((PAIRS * j + h) * P // 2) / (2.0 * math.pi)
+                nc.vector.tensor_scalar_mul(
+                    out=turns[:, h, j : j + 1],
+                    in0=turned[:, 1, 0:1],
+                    scalar1=first if j == 1 else -first,
+                )
+
+        table = const.tile([P, PAIRS, 2, 2, SEQ], F32)
+
+        def table_stage(span, h, stage_no, kept):
+            cols = slice(span * TOKENS, (span + 1) * TOKENS)
+            if stage_no == 0:
+                whole = angle.tile([P, 2, TOKENS], I32)
+                part = angle.tile([P, 2, TOKENS], F32)
+                for j in range(2):
+                    nc.vector.tensor_scalar_mul(
+                        out=whole[:, j, :], in0=position[:, cols], scalar1=turns[:, h, j : j + 1]
+                    )
+                    nc.vector.scalar_tensor_tensor(
+                        out=part[:, j, :],
+                        in0=position[:, cols],
+                        scalar=turns[:, h, j : j + 1],
+                        in1=whole[:, j, :],
+                        op0=ALU.mult,
+                        op1=ALU.subtract,
+                    )
+                for j in range(2):
+                    nc.scalar.activation(
+                        out=table[:, h, 1 - j, j, cols], in_=part[:, j, :], func=ACT.Sin, scale=2.0 * math.pi
+                    )
+                kept[0] = part
+            if stage_no == 1:
+                size = angle.tile([P, 2, TOKENS], F32)
+                nc.scalar.activation(out=size[:], in_=kept[0][:], func=ACT.Abs)
+                kept[1] = size
+            if stage_no == 2:
+                nc.scalar.activation(
+                    out=table[:, h].rearrange("p a b s -> p (a b) s")[:, 0:4:3, cols],
+                    in_=kept[1][:],
+                    func=ACT.Sin,
+                    scale=-2.0 * math.pi,
+                    bias=quarter_turn[:, 0:1],
+                )
+
+        def build_tables(span, h):
+            kept = {}
+            for stage_no in range(3):
+                table_stage(span, h, stage_no, kept)
+
+        build_tables(0, 0)
+
+        bias_rows_f32 = const.tile([P, P], F32)
+        nc.vector.tensor_copy(out=bias_rows_f32[:], in_=bias_rows[:])
+        nc.tensor.transpose(turned[:, 0, :], bias_rows_f32[:], ident[:])
+        bias = const.tile([P, 2 * TILES], F32)
+        nc.vector.tensor_copy(out=bias[:], in_=turned[:, 0, 0 : 2 * TILES])
+
+        def quantise_x(x_rows):
+            grouped = x_mx.tile([P, 4 * TOKENS], BF16, align_bytes=64)
+            for c in range(BLOCKS // 2):
+                turn_x(x_rows, grouped, c)
+            return quantise(grouped)
+
+        def turn_x(x_rows, grouped, c):
+            grouped_words = grouped[:].bitcast(F32).rearrange(
+                "p (c n m u) -> p c n m u", c=BLOCKS // 2, n=2, u=2
+            )
+            planes = turn_ps.tile([P, 2, 2, P], F32, name="bank", tag="bank")
+            for n in range(2):
+                words = x_rows[:, 2 * c + n, :].bitcast(F32)
+                for u in range(2):
+                    nc.tensor.transpose(planes[:, n, u, :], words[:, u:WORDS:2], ident[:])
+            nc.scalar.copy(out=grouped_words[:, c], in_=planes[:].rearrange("p n u m -> p n m u"))
+
+        def quantise(grouped):
+            codes = x_mx.tile([P, TOKENS], U32, align_bytes=64)
+            scales = x_mx.tile([P, TOKENS], U8, align_bytes=64)
+            nc.vector.quantize_mx(out=codes[:].bitcast(FP8X4), scales=scales[:], in_=grouped[:])
+            return codes, scales
+
+        def project(x_group, proj, h, lifted_soon):
+            codes, scales = x_group
+            lower = turn_ps.tile([P, TOKENS], F32, name="bank", tag="bank")
+            upper = turn_ps.tile([P, TOKENS], F32, name="bank", tag="bank")
+            for j, bank in enumerate((lower, upper)):
+                t = PAIRS * j + h
+                nc.tensor.matmul_mx(
+                    out=bank[:],
+                    lhsT=w_words[:, proj, 2 * P * t : 2 * P * (t + 1)].bitcast(FP4X4),
+                    lhsT_scale=w_scales[:, proj, P * t : P * (t + 1)],
+                    rhs=codes[:].bitcast(FP8X4),
+                    rhs_scale=scales[:],
+                    start=True,
+                    stop=True,
+                )
+            return lower, upper
+
+        def shared_products(banks, span, proj, h):
+            cols = slice(span * TOKENS, (span + 1) * TOKENS)
+            products = rotated.tile([P, 2, 2, TOKENS], F32)
+            t = TILES * proj + h
+            lower_sb = lifted.tile([P, TOKENS], F32)
+            nc.scalar.activation(
+                out=lower_sb[:], in_=banks[0][:], func=ACT.Identity, bias=bias[:, t : t + 1], scale=1.0
+            )
+            nc.gpsimd.tensor_tensor(
+                out=products[:, 0, :, :],
+                in0=lower_sb[:].unsqueeze(1).to_broadcast([P, 2, TOKENS]),
+                in1=table[:, h, 0, :, cols],
+                op=ALU.mult,
+            )
+            return products
+
+        def vector_products(banks, span, proj, h, products):
+            cols = slice(span * TOKENS, (span + 1) * TOKENS)
+            sources = (0, 1)
+            if products is None:
+                products = rotated.tile([P, 2, 2, TOKENS], F32)
+            else:
+                sources = (1,)
+            for source in sources:
+                t = TILES * proj + PAIRS * source + h
+                nc.vector.scalar_tensor_tensor(
+                    out=products[:, source, :, :],
+                    in0=banks[source][:].unsqueeze(1).to_broadcast([P, 2, TOKENS]),
+                    scalar=turned[:, 0, t : t + 1],
+                    in1=table[:, h, source, :, cols],
+                    op0=ALU.add,
+                    op1=ALU.mult,
+                )
+            return products
+
+        def add_halves(products):
+            nc.gpsimd.tensor_tensor(
+                out=products[:, 0, 0:SUMMED, :],
+                in0=products[:, 0, 0:SUMMED, :],
+                in1=products[:, 1, 0:SUMMED, :],
+                op=ALU.add,
+            )
+
+        def turn_back(products, h, stage, summed):
+            for j in (1, 0) if summed else (0, 1):
+                sums = turn_ps.tile([P, BLOCKS, P], F32, name="bank", tag="bank")
+                terms = 1 if (summed and j < SUMMED) else 2
+                for n in range(BLOCKS):
+                    for source in range(terms):
+                        nc.tensor.matmul(
+                            out=sums[:, n, :],
+                            lhsT=products[:, source, j, n * P : (n + 1) * P],
+                            rhs=ident[:],
+                            is_transpose=True,
+                            start=(source == 0),
+                            stop=(source == terms - 1),
+                        )
+                t = PAIRS * j + h
+                nc.scalar.copy(out=stage[:, :, t * P : (t + 1) * P], in_=sums[:])
+
+        steps = [(0, proj, h) for h in range(PAIRS) for proj in range(2)]
+        steps.extend(
+            (g, proj, h) for g in range(1, len(groups)) for proj in range(2) for h in range(PAIRS)
+        )
+        per_group = 2 * PAIRS // JOINED
+
+        def is_shared(i):
+            return i % 2 == 0
+
+        def is_summed(i):
+            return i % 2 == 1
+
+        x_of = {}
+        banks_of = {}
+        products_of = {}
+        stages = {}
+        halves = {}
+        later = {}
+
+        def front(m):
+            members = range(JOINED * m, JOINED * (m + 1))
+            for i in members:
+                g, proj, h = steps[i]
+                banks_of[i] = project(x_of[g], proj, h, is_shared(i))
+            for i in members:
+                g, proj, h = steps[i]
+                products_of[i] = None
+                if is_shared(i):
+                    products_of[i] = shared_products(banks_of[i], groups[g][1], proj, h)
+            for i in members:
+                g, proj, h = steps[i]
+                products_of[i] = vector_products(banks_of[i], groups[g][1], proj, h, products_of[i])
+            for i in members:
+                if is_summed(i):
+                    add_halves(products_of[i])
+
+        def back(m):
+            for i in range(JOINED * m, JOINED * (m + 1)):
+                g, proj, h = steps[i]
+                batch, span = groups[g]
+                if h == 0:
+                    stages[proj] = staging.tile([P, BLOCKS, FEAT], F32, name="stage")
+                turn_back(products_of[i], h, stages[proj], is_summed(i))
+                if h % 2 == 1:
+                    rows = outs[proj][batch, span * TOKENS : (span + 1) * TOKENS, :]
+                    rows = rows.rearrange("(n p) i -> p n i", p=P)
+                    for j in range(2):
+                        new = slice((PAIRS * j + h - 1) * P, (PAIRS * j + h + 1) * P)
+                        nc.sync.dma_start(out=rows[:, :, new], in_=stages[proj][:, :, new])
+
+        x_of[0] = quantise_x(loaded[0])
+        front(0)
+        build_tables(0, 1)
+        for m in range(len(steps) // JOINED):
+            g = steps[JOINED * m][0]
+            place = m % per_group
+            if place == 0 and g + 2 < len(groups):
+                loaded[g + 2] = load_x(g + 2)
+            if g + 1 < len(groups):
+                if place == 0:
+                    halves[0] = x_mx.tile([P, 4 * TOKENS], BF16, align_bytes=64, name="grouped")
+                if place < BLOCKS // 2:
+                    turn_x(loaded[g + 1], halves[0], place)
+                if place == BLOCKS // 2:
+                    x_of[g + 1] = quantise(halves[0])
+            if m + 1 < len(steps) // JOINED:
+                front(m + 1)
+            if m + 2 < PAIRS:
+                build_tables(0, m + 2)
+            if per_group <= m < per_group + 3 * PAIRS:
+                table_stage(1, (m - per_group) // 3, (m - per_group) % 3, later)
+            back(m)

@@ -20,11 +20,10 @@ ROPE_BASE = 10000.0
 TOKENS = 512
 BLOCKS = TOKENS // P
 SPANS = SEQ // TOKENS
-TILES = FEAT // P
-PAIRS = TILES // 2
+HALF = FEAT // 2
+WIDE = 2 * P
+TILES = HALF // WIDE
 WORDS = DIM // 2
-SUMMED = 1
-JOINED = 2
 
 FLOPS = 2 * BATCH * SEQ * DIM * 2 * FEAT
 
@@ -40,9 +39,9 @@ def tile_ropemultiheadattention_pa_t_kernel(
         angle = pools.enter_context(tc.tile_pool(name="angle", bufs=2))
         x_in = pools.enter_context(tc.tile_pool(name="x_in", bufs=3))
         x_mx = pools.enter_context(tc.tile_pool(name="x_mx", bufs=2))
-        rotated = pools.enter_context(tc.tile_pool(name="rotated", bufs=4))
+        rotated = pools.enter_context(tc.tile_pool(name="rotated", bufs=3))
         lifted = pools.enter_context(tc.tile_pool(name="lifted", bufs=2))
-        staging = pools.enter_context(tc.tile_pool(name="staging", bufs=4))
+        staging = pools.enter_context(tc.tile_pool(name="staging", bufs=6))
         keep_ps = pools.enter_context(tc.psum_pool(name="keep_ps", bufs=1))
         turn_ps = pools.enter_context(tc.psum_pool(name="turn_ps", bufs=7))
 
@@ -56,39 +55,58 @@ def tile_ropemultiheadattention_pa_t_kernel(
             return x_rows
 
         loaded = {0: load_x(0)}
-        bias_rows = const.tile([P, P], BF16)
+        rows_each = FEAT // WIDE
+        bias_rows = const.tile([P, WIDE], BF16)
         nc.vector.memset(bias_rows[:], 0.0)
-        nc.sync.dma_start(out=bias_rows[0:TILES, :], in_=bq.rearrange("(t p) -> t p", p=P))
-        nc.sync.dma_start(out=bias_rows[TILES : 2 * TILES, :], in_=bk.rearrange("(t p) -> t p", p=P))
-        w_words = const.tile([P, 2, 2 * FEAT], U8, align_bytes=64)
-        w_scales = const.tile([P, 2, FEAT], U8, align_bytes=64)
-        nc.vector.memset(w_scales[:].bitcast(I32), 0)
+        nc.sync.dma_start(out=bias_rows[0:rows_each, :], in_=bq.rearrange("(t p) -> t p", p=WIDE))
+        nc.sync.dma_start(out=bias_rows[rows_each : 2 * rows_each, :], in_=bk.rearrange("(t p) -> t p", p=WIDE))
+        raw_words = const.tile([P, 2, 2 * FEAT], U8, align_bytes=64)
+        raw_scales = const.tile([P, 2, FEAT], U8, align_bytes=64)
+        nc.vector.memset(raw_scales[:].bitcast(I32), 0)
         for proj, (words, scales) in enumerate(((Wq_words, Wq_scales), (Wk_words, Wk_scales))):
-            nc.sync.dma_start(out=w_words[:, proj, :].bitcast(I32), in_=words[0].bitcast(I32))
+            nc.sync.dma_start(out=raw_words[:, proj, :].bitcast(I32), in_=words[0].bitcast(I32))
             for quad in range(4):
                 nc.sync.dma_start(
-                    out=w_scales[32 * quad : 32 * quad + 4, proj, :].bitcast(I32),
+                    out=raw_scales[32 * quad : 32 * quad + 4, proj, :].bitcast(I32),
                     in_=scales[0, 4 * quad : 4 * quad + 4, :].bitcast(I32),
                 )
         loaded[1] = load_x(1)
+
+        w_words = const.tile([P, 2, 2, FEAT], U8, align_bytes=64)
+        w_scales = const.tile([P, 2, 2, HALF], U8, align_bytes=64)
+
+        def part_weights(proj, h):
+            for source in range(2):
+                first = HALF * source + WIDE * h
+                c = slice(first // 2, first // 2 + P)
+                nc.vector.tensor_copy(
+                    out=w_words[:, proj, :, 2 * c.start : 2 * c.stop].rearrange("p a (m b) -> p m a b", b=2),
+                    in_=raw_words[:, proj, 2 * first : 2 * (first + WIDE)].rearrange(
+                        "p (m a b) -> p m a b", a=2, b=2
+                    ),
+                )
+                nc.vector.tensor_copy(
+                    out=w_scales[:, proj, :, c].rearrange("p a m -> p m a"),
+                    in_=raw_scales[:, proj, first : first + WIDE].rearrange("p (m a) -> p m a", a=2),
+                )
 
         ident = const.tile([P, P], F32)
         make_identity(nc, ident[:])
 
         ratio = ROPE_BASE ** (-2.0 / FEAT)
         ratio_row = const.tile([P, P], F32)
-        nc.vector.memset(ratio_row[:, 0:2], 1.0)
-        width = 2
+        nc.vector.memset(ratio_row[:, 0:1], 1.0)
+        width = 1
         while width < P:
             nc.vector.tensor_scalar_mul(
                 out=ratio_row[:, width : 2 * width],
                 in0=ratio_row[:, 0:width],
-                scalar1=ratio ** (width // 2),
+                scalar1=ratio**width,
             )
             width *= 2
 
-        turned = keep_ps.tile([P, 2, P], F32)
-        nc.tensor.transpose(turned[:, 1, :], ratio_row[:], ident[:])
+        turned = keep_ps.tile([P, 3, P], F32)
+        nc.tensor.transpose(turned[:, 2, :], ratio_row[:], ident[:])
 
         position = const.tile([P, SEQ], F32)
         nc.gpsimd.iota(
@@ -100,17 +118,17 @@ def tile_ropemultiheadattention_pa_t_kernel(
         quarter_turn = const.tile([P, 1], F32)
         nc.vector.tensor_scalar_mul(out=quarter_turn[:], in0=quarter[:], scalar1=2.0 * math.pi)
 
-        turns = const.tile([P, PAIRS, 2], F32)
-        for h in range(PAIRS):
+        turns = const.tile([P, TILES, 2], F32)
+        for h in range(TILES):
             for j in range(2):
-                first = ratio ** ((PAIRS * j + h) * P // 2) / (2.0 * math.pi)
+                first = ratio ** ((HALF * j + WIDE * h) // 2) / (2.0 * math.pi)
                 nc.vector.tensor_scalar_mul(
                     out=turns[:, h, j : j + 1],
-                    in0=turned[:, 1, 0:1],
+                    in0=turned[:, 2, 0:1],
                     scalar1=first if j == 1 else -first,
                 )
 
-        table = const.tile([P, PAIRS, 2, 2, SEQ], F32)
+        table = const.tile([P, TILES, 2, 2, SEQ], F32)
 
         def table_stage(span, h, stage_no, kept):
             cols = slice(span * TOKENS, (span + 1) * TOKENS)
@@ -154,11 +172,12 @@ def tile_ropemultiheadattention_pa_t_kernel(
 
         build_tables(0, 0)
 
-        bias_rows_f32 = const.tile([P, P], F32)
-        nc.vector.tensor_copy(out=bias_rows_f32[:], in_=bias_rows[:])
-        nc.tensor.transpose(turned[:, 0, :], bias_rows_f32[:], ident[:])
-        bias = const.tile([P, 2 * TILES], F32)
-        nc.vector.tensor_copy(out=bias[:], in_=turned[:, 0, 0 : 2 * TILES])
+        bias_rows_f32 = const.tile([P, 2, P], F32)
+        nc.vector.tensor_copy(out=bias_rows_f32[:], in_=bias_rows[:].rearrange("t (m a) -> t a m", a=2))
+        for parity in range(2):
+            nc.tensor.transpose(turned[:, parity, :], bias_rows_f32[:, parity, :], ident[:])
+        bias = const.tile([P, 2 * rows_each], F32)
+        nc.vector.tensor_copy(out=bias[:], in_=turned[:, 0, 0 : 2 * rows_each])
 
         def quantise_x(x_rows):
             grouped = x_mx.tile([P, 4 * TOKENS], BF16, align_bytes=64)
@@ -183,138 +202,108 @@ def tile_ropemultiheadattention_pa_t_kernel(
             nc.vector.quantize_mx(out=codes[:].bitcast(FP8X4), scales=scales[:], in_=grouped[:])
             return codes, scales
 
-        def project(x_group, proj, h, lifted_soon):
+        def project(x_group, proj, h, parity, source):
             codes, scales = x_group
-            lower = turn_ps.tile([P, TOKENS], F32, name="bank", tag="bank")
-            upper = turn_ps.tile([P, TOKENS], F32, name="bank", tag="bank")
-            for j, bank in enumerate((lower, upper)):
-                t = PAIRS * j + h
-                nc.tensor.matmul_mx(
-                    out=bank[:],
-                    lhsT=w_words[:, proj, 2 * P * t : 2 * P * (t + 1)].bitcast(FP4X4),
-                    lhsT_scale=w_scales[:, proj, P * t : P * (t + 1)],
-                    rhs=codes[:].bitcast(FP8X4),
-                    rhs_scale=scales[:],
-                    start=True,
-                    stop=True,
-                )
-            return lower, upper
-
-        def shared_products(banks, span, proj, h):
-            cols = slice(span * TOKENS, (span + 1) * TOKENS)
-            products = rotated.tile([P, 2, 2, TOKENS], F32)
-            t = TILES * proj + h
-            lower_sb = lifted.tile([P, TOKENS], F32)
-            nc.scalar.activation(
-                out=lower_sb[:], in_=banks[0][:], func=ACT.Identity, bias=bias[:, t : t + 1], scale=1.0
+            bank = turn_ps.tile([P, TOKENS], F32, name="bank", tag="bank")
+            c = (HALF * source + WIDE * h) // 2
+            nc.tensor.matmul_mx(
+                out=bank[:],
+                lhsT=w_words[:, proj, parity, 2 * c : 2 * (c + P)].bitcast(FP4X4),
+                lhsT_scale=w_scales[:, proj, parity, c : c + P],
+                rhs=codes[:].bitcast(FP8X4),
+                rhs_scale=scales[:],
+                start=True,
+                stop=True,
             )
-            nc.gpsimd.tensor_tensor(
-                out=products[:, 0, :, :],
-                in0=lower_sb[:].unsqueeze(1).to_broadcast([P, 2, TOKENS]),
-                in1=table[:, h, 0, :, cols],
-                op=ALU.mult,
-            )
-            return products
+            return bank
 
-        def vector_products(banks, span, proj, h, products):
-            cols = slice(span * TOKENS, (span + 1) * TOKENS)
-            sources = (0, 1)
-            if products is None:
-                products = rotated.tile([P, 2, 2, TOKENS], F32)
-            else:
-                sources = (1,)
-            for source in sources:
-                t = TILES * proj + PAIRS * source + h
-                nc.vector.scalar_tensor_tensor(
-                    out=products[:, source, :, :],
-                    in0=banks[source][:].unsqueeze(1).to_broadcast([P, 2, TOKENS]),
-                    scalar=turned[:, 0, t : t + 1],
-                    in1=table[:, h, source, :, cols],
-                    op0=ALU.add,
-                    op1=ALU.mult,
-                )
-            return products
-
-        def add_halves(products):
-            nc.gpsimd.tensor_tensor(
-                out=products[:, 0, 0:SUMMED, :],
-                in0=products[:, 0, 0:SUMMED, :],
-                in1=products[:, 1, 0:SUMMED, :],
-                op=ALU.add,
-            )
-
-        def turn_back(products, h, stage, summed):
-            for j in (1, 0) if summed else (0, 1):
-                sums = turn_ps.tile([P, BLOCKS, P], F32, name="bank", tag="bank")
-                terms = 1 if (summed and j < SUMMED) else 2
-                for n in range(BLOCKS):
-                    for source in range(terms):
-                        nc.tensor.matmul(
-                            out=sums[:, n, :],
-                            lhsT=products[:, source, j, n * P : (n + 1) * P],
-                            rhs=ident[:],
-                            is_transpose=True,
-                            start=(source == 0),
-                            stop=(source == terms - 1),
-                        )
-                t = PAIRS * j + h
-                nc.scalar.copy(out=stage[:, :, t * P : (t + 1) * P], in_=sums[:])
-
-        steps = [(0, proj, h) for h in range(PAIRS) for proj in range(2)]
-        steps.extend(
-            (g, proj, h) for g in range(1, len(groups)) for proj in range(2) for h in range(PAIRS)
+        batches = [(0, proj, h) for h in range(TILES) for proj in range(2)]
+        batches.extend(
+            (g, proj, h) for g in range(1, len(groups)) for proj in range(2) for h in range(TILES)
         )
-        per_group = 2 * PAIRS // JOINED
-
-        def is_shared(i):
-            return i % 2 == 0
-
-        def is_summed(i):
-            return i % 2 == 1
+        per_group = 2 * TILES
 
         x_of = {}
-        banks_of = {}
         products_of = {}
-        stages = {}
         halves = {}
         later = {}
 
         def front(m):
-            members = range(JOINED * m, JOINED * (m + 1))
-            for i in members:
-                g, proj, h = steps[i]
-                banks_of[i] = project(x_of[g], proj, h, is_shared(i))
-            for i in members:
-                g, proj, h = steps[i]
-                products_of[i] = None
-                if is_shared(i):
-                    products_of[i] = shared_products(banks_of[i], groups[g][1], proj, h)
-            for i in members:
-                g, proj, h = steps[i]
-                products_of[i] = vector_products(banks_of[i], groups[g][1], proj, h, products_of[i])
-            for i in members:
-                if is_summed(i):
-                    add_halves(products_of[i])
+            g, proj, h = batches[m]
+            span = groups[g][1]
+            cols = slice(span * TOKENS, (span + 1) * TOKENS)
+            banks = {}
+            for parity in range(2):
+                for source in range(2):
+                    banks[parity, source] = project(x_of[g], proj, h, parity, source)
+            products = rotated.tile([P, 2, 2, 2, TOKENS], F32)
+            t = 2 * TILES * proj + h
+            lower_sb = lifted.tile([P, TOKENS], F32)
+            nc.scalar.activation(
+                out=lower_sb[:], in_=banks[0, 0][:], func=ACT.Identity, bias=bias[:, t : t + 1], scale=1.0
+            )
+            nc.gpsimd.tensor_tensor(
+                out=products[:, 0, 0, :, :],
+                in0=lower_sb[:].unsqueeze(1).to_broadcast([P, 2, TOKENS]),
+                in1=table[:, h, 0, :, cols],
+                op=ALU.mult,
+            )
+            for parity, source in ((0, 1), (1, 0), (1, 1)):
+                t = 2 * TILES * proj + TILES * source + h
+                nc.vector.scalar_tensor_tensor(
+                    out=products[:, parity, source, :, :],
+                    in0=banks[parity, source][:].unsqueeze(1).to_broadcast([P, 2, TOKENS]),
+                    scalar=turned[:, parity, t : t + 1],
+                    in1=table[:, h, source, :, cols],
+                    op0=ALU.add,
+                    op1=ALU.mult,
+                )
+            late = slice(TOKENS // 2, TOKENS)
+            nc.gpsimd.tensor_tensor(
+                out=products[:, :, 0, 0, late],
+                in0=products[:, :, 0, 0, late],
+                in1=products[:, :, 1, 0, late],
+                op=ALU.add,
+            )
+            products_of[m] = products
 
         def back(m):
-            for i in range(JOINED * m, JOINED * (m + 1)):
-                g, proj, h = steps[i]
-                batch, span = groups[g]
-                if h == 0:
-                    stages[proj] = staging.tile([P, BLOCKS, FEAT], F32, name="stage")
-                turn_back(products_of[i], h, stages[proj], is_summed(i))
-                if h % 2 == 1:
-                    rows = outs[proj][batch, span * TOKENS : (span + 1) * TOKENS, :]
-                    rows = rows.rearrange("(n p) i -> p n i", p=P)
-                    for j in range(2):
-                        new = slice((PAIRS * j + h - 1) * P, (PAIRS * j + h + 1) * P)
-                        nc.sync.dma_start(out=rows[:, :, new], in_=stages[proj][:, :, new])
+            g, proj, h = batches[m]
+            batch, span = groups[g]
+            products = products_of[m]
+            rows = outs[proj][batch, span * TOKENS : (span + 1) * TOKENS, :]
+            rows = rows.rearrange("(n p) i -> p n i", p=P)
+            for j in (1, 0):
+                stage = staging.tile([P, BLOCKS, WIDE], F32, name="stage")
+                for c in range(BLOCKS // 2):
+                    sums = turn_ps.tile([P, 2, 2, P], F32, name="bank", tag="bank")
+                    terms = 1 if (j == 0 and c == BLOCKS // 2 - 1) else 2
+                    for n in range(2):
+                        first = (2 * c + n) * P
+                        for parity in range(2):
+                            for source in range(terms):
+                                nc.tensor.matmul(
+                                    out=sums[:, n, parity, :],
+                                    lhsT=products[:, parity, source, j, first : first + P],
+                                    rhs=ident[:],
+                                    is_transpose=True,
+                                    start=(source == 0),
+                                    stop=(source == terms - 1),
+                                )
+                    nc.scalar.copy(
+                        out=stage[:, 2 * c : 2 * c + 2, :].rearrange("p n (m a) -> p n m a", a=2),
+                        in_=sums[:].rearrange("p n a m -> p n m a"),
+                    )
+                new = HALF * j + WIDE * h
+                nc.sync.dma_start(out=rows[:, :, new : new + WIDE], in_=stage[:])
 
         x_of[0] = quantise_x(loaded[0])
+        part_weights(0, 0)
         front(0)
+        part_weights(1, 0)
         build_tables(0, 1)
-        for m in range(len(steps) // JOINED):
-            g = steps[JOINED * m][0]
+        for m in range(len(batches)):
+            g = batches[m][0]
             place = m % per_group
             if place == 0 and g + 2 < len(groups):
                 loaded[g + 2] = load_x(g + 2)
@@ -325,10 +314,11 @@ def tile_ropemultiheadattention_pa_t_kernel(
                     turn_x(loaded[g + 1], halves[0], place)
                 if place == BLOCKS // 2:
                     x_of[g + 1] = quantise(halves[0])
-            if m + 1 < len(steps) // JOINED:
+            if m + 1 < len(batches):
                 front(m + 1)
-            if m + 2 < PAIRS:
-                build_tables(0, m + 2)
-            if per_group <= m < per_group + 3 * PAIRS:
-                table_stage(1, (m - per_group) // 3, (m - per_group) % 3, later)
+            if m < 2:
+                part_weights(m, 1)
+            if per_group <= m < 4 * per_group and m % 2 == 0:
+                stage_no = (m - per_group) // 2
+                table_stage(1, stage_no // 3, stage_no % 3, later)
             back(m)

@@ -23,6 +23,8 @@ SPANS = SEQ // TOKENS
 HALF = FEAT // 2
 WIDE = 2 * P
 TILES = HALF // WIDE
+EDGE_PIECES = 2
+EDGE_TOKENS = TOKENS // EDGE_PIECES
 WORDS = DIM // 2
 
 FLOPS = 2 * BATCH * SEQ * DIM * 2 * FEAT
@@ -47,14 +49,16 @@ def tile_ropemultiheadattention_pa_t_kernel(
 
         groups = [(batch, span) for span in range(SPANS) for batch in range(BATCH)]
 
-        def load_x(g):
+        def load_x(g, parts=1):
             batch, span = groups[g]
-            rows = x[batch, span * TOKENS : (span + 1) * TOKENS, :]
+            rows = x[batch, span * TOKENS : (span + 1) * TOKENS, :].rearrange("(n p) k -> p n k", p=P)
             x_rows = x_in.tile([P, BLOCKS, DIM], BF16)
-            nc.sync.dma_start(out=x_rows[:], in_=rows.rearrange("(n p) k -> p n k", p=P))
+            for part in range(parts):
+                some = slice(part * BLOCKS // parts, (part + 1) * BLOCKS // parts)
+                nc.sync.dma_start(out=x_rows[:, some, :], in_=rows[:, some, :])
             return x_rows
 
-        loaded = {0: load_x(0)}
+        loaded = {0: load_x(0, EDGE_PIECES)}
         rows_each = FEAT // WIDE
         bias_rows = const.tile([P, WIDE], BF16)
         nc.vector.memset(bias_rows[:], 0.0)
@@ -130,11 +134,11 @@ def tile_ropemultiheadattention_pa_t_kernel(
 
         table = const.tile([P, TILES, 2, 2, SEQ], F32)
 
-        def table_stage(span, h, stage_no, kept):
-            cols = slice(span * TOKENS, (span + 1) * TOKENS)
+        def table_stage(first, width, h, stage_no, kept):
+            cols = slice(first, first + width)
             if stage_no == 0:
-                whole = angle.tile([P, 2, TOKENS], I32)
-                part = angle.tile([P, 2, TOKENS], F32)
+                whole = angle.tile([P, 2, width], I32)
+                part = angle.tile([P, 2, width], F32)
                 for j in range(2):
                     nc.vector.tensor_scalar_mul(
                         out=whole[:, j, :], in0=position[:, cols], scalar1=turns[:, h, j : j + 1]
@@ -153,7 +157,7 @@ def tile_ropemultiheadattention_pa_t_kernel(
                     )
                 kept[0] = part
             if stage_no == 1:
-                size = angle.tile([P, 2, TOKENS], F32)
+                size = angle.tile([P, 2, width], F32)
                 nc.scalar.activation(out=size[:], in_=kept[0][:], func=ACT.Abs)
                 kept[1] = size
             if stage_no == 2:
@@ -165,12 +169,12 @@ def tile_ropemultiheadattention_pa_t_kernel(
                     bias=quarter_turn[:, 0:1],
                 )
 
-        def build_tables(span, h):
+        def build_tables(first, width, h):
             kept = {}
             for stage_no in range(3):
-                table_stage(span, h, stage_no, kept)
+                table_stage(first, width, h, stage_no, kept)
 
-        build_tables(0, 0)
+        build_tables(0, EDGE_TOKENS, 0)
 
         bias_rows_f32 = const.tile([P, 2, P], F32)
         nc.vector.tensor_copy(out=bias_rows_f32[:], in_=bias_rows[:].rearrange("t (m a) -> t a m", a=2))
@@ -178,12 +182,6 @@ def tile_ropemultiheadattention_pa_t_kernel(
             nc.tensor.transpose(turned[:, parity, :], bias_rows_f32[:, parity, :], ident[:])
         bias = const.tile([P, 2 * rows_each], F32)
         nc.vector.tensor_copy(out=bias[:], in_=turned[:, 0, 0 : 2 * rows_each])
-
-        def quantise_x(x_rows):
-            grouped = x_mx.tile([P, 4 * TOKENS], BF16, align_bytes=64)
-            for c in range(BLOCKS // 2):
-                turn_x(x_rows, grouped, c)
-            return quantise(grouped)
 
         def turn_x(x_rows, grouped, c):
             grouped_words = grouped[:].bitcast(F32).rearrange(
@@ -196,22 +194,28 @@ def tile_ropemultiheadattention_pa_t_kernel(
                     nc.tensor.transpose(planes[:, n, u, :], words[:, u:WORDS:2], ident[:])
             nc.scalar.copy(out=grouped_words[:, c], in_=planes[:].rearrange("p n u m -> p n m u"))
 
-        def quantise(grouped):
+        def quantise(grouped, codes, scales, some=slice(0, TOKENS)):
+            nc.vector.quantize_mx(
+                out=codes[:, some].bitcast(FP8X4),
+                scales=scales[:, some],
+                in_=grouped[:, 4 * some.start : 4 * some.stop],
+            )
+
+        def new_codes():
             codes = x_mx.tile([P, TOKENS], U32, align_bytes=64)
             scales = x_mx.tile([P, TOKENS], U8, align_bytes=64)
-            nc.vector.quantize_mx(out=codes[:].bitcast(FP8X4), scales=scales[:], in_=grouped[:])
             return codes, scales
 
-        def project(x_group, proj, h, parity, source):
+        def project(x_group, proj, h, parity, source, some):
             codes, scales = x_group
             bank = turn_ps.tile([P, TOKENS], F32, name="bank", tag="bank")
             c = (HALF * source + WIDE * h) // 2
             nc.tensor.matmul_mx(
-                out=bank[:],
+                out=bank[:, 0 : some.stop - some.start],
                 lhsT=w_words[:, proj, parity, 2 * c : 2 * (c + P)].bitcast(FP4X4),
                 lhsT_scale=w_scales[:, proj, parity, c : c + P],
-                rhs=codes[:].bitcast(FP8X4),
-                rhs_scale=scales[:],
+                rhs=codes[:, some].bitcast(FP8X4),
+                rhs_scale=scales[:, some],
                 start=True,
                 stop=True,
             )
@@ -228,44 +232,52 @@ def tile_ropemultiheadattention_pa_t_kernel(
         halves = {}
         later = {}
 
-        def front(m):
+        def is_edge(m):
+            return m == 0 or m == len(batches) - 1
+
+        def front(m, some=slice(0, TOKENS)):
             g, proj, h = batches[m]
-            span = groups[g][1]
-            cols = slice(span * TOKENS, (span + 1) * TOKENS)
+            width = some.stop - some.start
+            cols = slice(groups[g][1] * TOKENS + some.start, groups[g][1] * TOKENS + some.stop)
             banks = {}
             for parity in range(2):
                 for source in range(2):
-                    banks[parity, source] = project(x_of[g], proj, h, parity, source)
-            products = rotated.tile([P, 2, 2, 2, TOKENS], F32)
+                    banks[parity, source] = project(x_of[g], proj, h, parity, source, some)
+            if some.start == 0:
+                products_of[m] = rotated.tile([P, 2, 2, 2, TOKENS], F32, name="products")
+            products = products_of[m]
             t = 2 * TILES * proj + h
             lower_sb = lifted.tile([P, TOKENS], F32)
             nc.scalar.activation(
-                out=lower_sb[:], in_=banks[0, 0][:], func=ACT.Identity, bias=bias[:, t : t + 1], scale=1.0
+                out=lower_sb[:, 0:width],
+                in_=banks[0, 0][:, 0:width],
+                func=ACT.Identity,
+                bias=bias[:, t : t + 1],
+                scale=1.0,
             )
             nc.gpsimd.tensor_tensor(
-                out=products[:, 0, 0, :, :],
-                in0=lower_sb[:].unsqueeze(1).to_broadcast([P, 2, TOKENS]),
+                out=products[:, 0, 0, :, some],
+                in0=lower_sb[:, 0:width].unsqueeze(1).to_broadcast([P, 2, width]),
                 in1=table[:, h, 0, :, cols],
                 op=ALU.mult,
             )
             for parity, source in ((0, 1), (1, 0), (1, 1)):
                 t = 2 * TILES * proj + TILES * source + h
                 nc.vector.scalar_tensor_tensor(
-                    out=products[:, parity, source, :, :],
-                    in0=banks[parity, source][:].unsqueeze(1).to_broadcast([P, 2, TOKENS]),
+                    out=products[:, parity, source, :, some],
+                    in0=banks[parity, source][:, 0:width].unsqueeze(1).to_broadcast([P, 2, width]),
                     scalar=turned[:, parity, t : t + 1],
                     in1=table[:, h, source, :, cols],
                     op0=ALU.add,
                     op1=ALU.mult,
                 )
-            late = slice(TOKENS // 2, TOKENS)
-            nc.gpsimd.tensor_tensor(
-                out=products[:, :, 0, 0, late],
-                in0=products[:, :, 0, 0, late],
-                in1=products[:, :, 1, 0, late],
-                op=ALU.add,
-            )
-            products_of[m] = products
+            if not is_edge(m):
+                nc.gpsimd.tensor_tensor(
+                    out=products[:, 0, 0, 0, :],
+                    in0=products[:, 0, 0, 0, :],
+                    in1=products[:, 0, 1, 0, :],
+                    op=ALU.add,
+                )
 
         def back(m):
             g, proj, h = batches[m]
@@ -273,35 +285,48 @@ def tile_ropemultiheadattention_pa_t_kernel(
             products = products_of[m]
             rows = outs[proj][batch, span * TOKENS : (span + 1) * TOKENS, :]
             rows = rows.rearrange("(n p) i -> p n i", p=P)
-            for j in (1, 0):
-                stage = staging.tile([P, BLOCKS, WIDE], F32, name="stage")
-                for c in range(BLOCKS // 2):
-                    sums = turn_ps.tile([P, 2, 2, P], F32, name="bank", tag="bank")
-                    terms = 1 if (j == 0 and c == BLOCKS // 2 - 1) else 2
-                    for n in range(2):
-                        first = (2 * c + n) * P
-                        for parity in range(2):
-                            for source in range(terms):
-                                nc.tensor.matmul(
-                                    out=sums[:, n, parity, :],
-                                    lhsT=products[:, parity, source, j, first : first + P],
-                                    rhs=ident[:],
-                                    is_transpose=True,
-                                    start=(source == 0),
-                                    stop=(source == terms - 1),
-                                )
-                    nc.scalar.copy(
-                        out=stage[:, 2 * c : 2 * c + 2, :].rearrange("p n (m a) -> p n m a", a=2),
-                        in_=sums[:].rearrange("p n a m -> p n m a"),
-                    )
-                new = HALF * j + WIDE * h
-                nc.sync.dma_start(out=rows[:, :, new : new + WIDE], in_=stage[:])
+            stages = [staging.tile([P, BLOCKS, WIDE], F32, name="stage") for j in range(2)]
+            banks = [(j, c) for j in (1, 0) for c in range(2)]
+            if is_edge(m):
+                banks = [(j, c) for c in range(2) for j in (1, 0)]
+            for j, c in banks:
+                some = slice(2 * c, 2 * c + 2)
+                sums = turn_ps.tile([P, 2, 2, P], F32, name="bank", tag="bank")
+                for n in range(2):
+                    first = (2 * c + n) * P
+                    for parity in range(2):
+                        terms = 1 if (j == 0 and parity == 0 and not is_edge(m)) else 2
+                        for source in range(terms):
+                            nc.tensor.matmul(
+                                out=sums[:, n, parity, :],
+                                lhsT=products[:, parity, source, j, first : first + P],
+                                rhs=ident[:],
+                                is_transpose=True,
+                                start=(source == 0),
+                                stop=(source == terms - 1),
+                            )
+                nc.scalar.copy(
+                    out=stages[j][:, some, :].rearrange("p n (m a) -> p n m a", a=2),
+                    in_=sums[:].rearrange("p n a m -> p n m a"),
+                )
+                new = slice(HALF * j + WIDE * h, HALF * j + WIDE * (h + 1))
+                if is_edge(m):
+                    nc.sync.dma_start(out=rows[:, some, new], in_=stages[j][:, some, :])
+                elif c == 1:
+                    nc.sync.dma_start(out=rows[:, :, new], in_=stages[j][:])
 
-        x_of[0] = quantise_x(loaded[0])
         part_weights(0, 0)
-        front(0)
+        grouped = x_mx.tile([P, 4 * TOKENS], BF16, align_bytes=64)
+        x_of[0] = new_codes()
+        for piece in range(EDGE_PIECES):
+            some = slice(piece * EDGE_TOKENS, (piece + 1) * EDGE_TOKENS)
+            turn_x(loaded[0], grouped, piece)
+            quantise(grouped, *x_of[0], some)
+            if piece > 0:
+                build_tables(some.start, EDGE_TOKENS, 0)
+            front(0, some)
         part_weights(1, 0)
-        build_tables(0, 1)
+        build_tables(0, TOKENS, 1)
         for m in range(len(batches)):
             g = batches[m][0]
             place = m % per_group
@@ -313,12 +338,17 @@ def tile_ropemultiheadattention_pa_t_kernel(
                 if place < BLOCKS // 2:
                     turn_x(loaded[g + 1], halves[0], place)
                 if place == BLOCKS // 2:
-                    x_of[g + 1] = quantise(halves[0])
+                    x_of[g + 1] = new_codes()
+                    quantise(halves[0], *x_of[g + 1])
             if m + 1 < len(batches):
-                front(m + 1)
+                if is_edge(m + 1):
+                    for piece in range(EDGE_PIECES):
+                        front(m + 1, slice(piece * EDGE_TOKENS, (piece + 1) * EDGE_TOKENS))
+                else:
+                    front(m + 1)
             if m < 2:
                 part_weights(m, 1)
             if per_group <= m < 4 * per_group and m % 2 == 0:
                 stage_no = (m - per_group) // 2
-                table_stage(1, stage_no // 3, stage_no % 3, later)
+                table_stage(TOKENS, TOKENS, stage_no // 3, stage_no % 3, later)
             back(m)

@@ -25,6 +25,7 @@ WIDE = 2 * P
 TILES = HALF // WIDE
 EDGE_PIECES = 2
 EDGE_TOKENS = TOKENS // EDGE_PIECES
+STAGES = 6
 WORDS = DIM // 2
 
 FLOPS = 2 * BATCH * SEQ * DIM * 2 * FEAT
@@ -49,32 +50,32 @@ def tile_ropemultiheadattention_pa_t_kernel(
 
         groups = [(batch, span) for span in range(SPANS) for batch in range(BATCH)]
 
-        def load_x(g, parts=1):
+        def load_x(g, x_rows, first=0, last=BLOCKS):
             batch, span = groups[g]
             rows = x[batch, span * TOKENS : (span + 1) * TOKENS, :].rearrange("(n p) k -> p n k", p=P)
-            x_rows = x_in.tile([P, BLOCKS, DIM], BF16)
-            for part in range(parts):
-                some = slice(part * BLOCKS // parts, (part + 1) * BLOCKS // parts)
-                nc.sync.dma_start(out=x_rows[:, some, :], in_=rows[:, some, :])
-            return x_rows
+            nc.sync.dma_start(out=x_rows[:, first:last, :], in_=rows[:, first:last, :])
 
-        loaded = {0: load_x(0, EDGE_PIECES)}
-        rows_each = FEAT // WIDE
-        bias_rows = const.tile([P, WIDE], BF16)
-        nc.vector.memset(bias_rows[:], 0.0)
-        nc.sync.dma_start(out=bias_rows[0:rows_each, :], in_=bq.rearrange("(t p) -> t p", p=WIDE))
-        nc.sync.dma_start(out=bias_rows[rows_each : 2 * rows_each, :], in_=bk.rearrange("(t p) -> t p", p=WIDE))
         raw_words = const.tile([P, 2, 2 * FEAT], U8, align_bytes=64)
         raw_scales = const.tile([P, 2, FEAT], U8, align_bytes=64)
         nc.vector.memset(raw_scales[:].bitcast(I32), 0)
-        for proj, (words, scales) in enumerate(((Wq_words, Wq_scales), (Wk_words, Wk_scales))):
-            nc.sync.dma_start(out=raw_words[:, proj, :].bitcast(I32), in_=words[0].bitcast(I32))
+        loaded = {0: x_in.tile([P, BLOCKS, DIM], BF16, name="x_rows")}
+        load_x(0, loaded[0], 0, BLOCKS // 2)
+        for proj, scales in enumerate((Wq_scales, Wk_scales)):
             for quad in range(4):
                 nc.sync.dma_start(
                     out=raw_scales[32 * quad : 32 * quad + 4, proj, :].bitcast(I32),
                     in_=scales[0, 4 * quad : 4 * quad + 4, :].bitcast(I32),
                 )
-        loaded[1] = load_x(1)
+        nc.sync.dma_start(out=raw_words[:, 0, :].bitcast(I32), in_=Wq_words[0].bitcast(I32))
+        rows_each = FEAT // WIDE
+        bias_rows = const.tile([P, WIDE], BF16)
+        nc.vector.memset(bias_rows[:], 0.0)
+        nc.sync.dma_start(out=bias_rows[0:rows_each, :], in_=bq.rearrange("(t p) -> t p", p=WIDE))
+        nc.sync.dma_start(out=bias_rows[rows_each : 2 * rows_each, :], in_=bk.rearrange("(t p) -> t p", p=WIDE))
+        load_x(0, loaded[0], BLOCKS // 2, BLOCKS)
+        nc.sync.dma_start(out=raw_words[:, 1, :].bitcast(I32), in_=Wk_words[0].bitcast(I32))
+        loaded[1] = x_in.tile([P, BLOCKS, DIM], BF16, name="x_rows")
+        load_x(1, loaded[1])
 
         w_words = const.tile([P, 2, 2, FEAT], U8, align_bytes=64)
         w_scales = const.tile([P, 2, 2, HALF], U8, align_bytes=64)
@@ -136,34 +137,36 @@ def tile_ropemultiheadattention_pa_t_kernel(
 
         def table_stage(first, width, h, stage_no, kept):
             cols = slice(first, first + width)
+            kind, j = divmod(stage_no, 2)
             if stage_no == 0:
                 whole = angle.tile([P, 2, width], I32)
                 part = angle.tile([P, 2, width], F32)
-                for j in range(2):
+                size = angle.tile([P, 2, width], F32)
+                for half in range(2):
                     nc.vector.tensor_scalar_mul(
-                        out=whole[:, j, :], in0=position[:, cols], scalar1=turns[:, h, j : j + 1]
+                        out=whole[:, half, :], in0=position[:, cols], scalar1=turns[:, h, half : half + 1]
                     )
                     nc.vector.scalar_tensor_tensor(
-                        out=part[:, j, :],
+                        out=part[:, half, :],
                         in0=position[:, cols],
-                        scalar=turns[:, h, j : j + 1],
-                        in1=whole[:, j, :],
+                        scalar=turns[:, h, half : half + 1],
+                        in1=whole[:, half, :],
                         op0=ALU.mult,
                         op1=ALU.subtract,
                     )
-                for j in range(2):
-                    nc.scalar.activation(
-                        out=table[:, h, 1 - j, j, cols], in_=part[:, j, :], func=ACT.Sin, scale=2.0 * math.pi
-                    )
-                kept[0] = part
-            if stage_no == 1:
-                size = angle.tile([P, 2, width], F32)
-                nc.scalar.activation(out=size[:], in_=kept[0][:], func=ACT.Abs)
-                kept[1] = size
-            if stage_no == 2:
+                kept["part"] = part
+                kept["size"] = size
+            part, size = kept["part"], kept["size"]
+            if kind == 0:
                 nc.scalar.activation(
-                    out=table[:, h].rearrange("p a b s -> p (a b) s")[:, 0:4:3, cols],
-                    in_=kept[1][:],
+                    out=table[:, h, 1 - j, j, cols], in_=part[:, j, :], func=ACT.Sin, scale=2.0 * math.pi
+                )
+            if kind == 1:
+                nc.scalar.activation(out=size[:, j, :], in_=part[:, j, :], func=ACT.Abs)
+            if kind == 2:
+                nc.scalar.activation(
+                    out=table[:, h, j, j, cols],
+                    in_=size[:, j, :],
                     func=ACT.Sin,
                     scale=-2.0 * math.pi,
                     bias=quarter_turn[:, 0:1],
@@ -171,7 +174,7 @@ def tile_ropemultiheadattention_pa_t_kernel(
 
         def build_tables(first, width, h):
             kept = {}
-            for stage_no in range(3):
+            for stage_no in range(STAGES):
                 table_stage(first, width, h, stage_no, kept)
 
         build_tables(0, EDGE_TOKENS, 0)
@@ -331,7 +334,14 @@ def tile_ropemultiheadattention_pa_t_kernel(
             g = batches[m][0]
             place = m % per_group
             if place == 0 and g + 2 < len(groups):
-                loaded[g + 2] = load_x(g + 2)
+                loaded[g + 2] = x_in.tile([P, BLOCKS, DIM], BF16, name="x_rows")
+                load_x(g + 2, loaded[g + 2])
+            if m + 1 < len(batches):
+                if is_edge(m + 1):
+                    for piece in range(EDGE_PIECES):
+                        front(m + 1, slice(piece * EDGE_TOKENS, (piece + 1) * EDGE_TOKENS))
+                else:
+                    front(m + 1)
             if g + 1 < len(groups):
                 if place == 0:
                     halves[0] = x_mx.tile([P, 4 * TOKENS], BF16, align_bytes=64, name="grouped")
@@ -340,15 +350,8 @@ def tile_ropemultiheadattention_pa_t_kernel(
                 if place == BLOCKS // 2:
                     x_of[g + 1] = new_codes()
                     quantise(halves[0], *x_of[g + 1])
-            if m + 1 < len(batches):
-                if is_edge(m + 1):
-                    for piece in range(EDGE_PIECES):
-                        front(m + 1, slice(piece * EDGE_TOKENS, (piece + 1) * EDGE_TOKENS))
-                else:
-                    front(m + 1)
             if m < 2:
                 part_weights(m, 1)
-            if per_group <= m < 4 * per_group and m % 2 == 0:
-                stage_no = (m - per_group) // 2
-                table_stage(TOKENS, TOKENS, stage_no // 3, stage_no % 3, later)
+            if 3 <= m < 3 + TILES * STAGES:
+                table_stage(TOKENS, TOKENS, (m - 3) // STAGES, (m - 3) % STAGES, later)
             back(m)

import math
from contextlib import ExitStack

import concourse.mybir as mybir
from concourse.masks import make_identity

F32 = mybir.dt.float32
BF16 = mybir.dt.bfloat16
I32 = mybir.dt.int32
U32 = mybir.dt.uint32
U8 = mybir.dt.uint8
FP8X4 = mybir.dt.float8_e4m3fn_x4
FP4X4 = mybir.dt.float4_e2m1fn_x4
ALU = mybir.AluOpType
ACT = mybir.ActivationFunctionType

P = 128
BATCH, SEQ, DIM, FEAT = 4, 1024, 512, 1024
ROPE_BASE = 10000.0
TOKENS = 512
BLOCKS = TOKENS // P
SPANS = SEQ // TOKENS
HALF = FEAT // 2
WIDE = 2 * P
TILES = HALF // WIDE
EDGE_PIECES = 2
EDGE_TOKENS = TOKENS // EDGE_PIECES
STAGES = 6
WORDS = DIM // 2

FLOPS = 2 * BATCH * SEQ * DIM * 2 * FEAT


def tile_ropemultiheadattention_pa_t_kernel(
    tc, x, Wq_words, Wq_scales, bq, Wk_words, Wk_scales, bk, out_0, out_1
):
    nc = tc.nc
    outs = (out_0, out_1)

    with ExitStack() as pools:
        const = pools.enter_context(tc.tile_pool(name="const", bufs=1))
        angle = pools.enter_context(tc.tile_pool(name="angle", bufs=2))
        x_in = pools.enter_context(tc.tile_pool(name="x_in", bufs=3))
        x_mx = pools.enter_context(tc.tile_pool(name="x_mx", bufs=2))
        rotated = pools.enter_context(tc.tile_pool(name="rotated", bufs=3))
        lifted = pools.enter_context(tc.tile_pool(name="lifted", bufs=2))
        staging = pools.enter_context(tc.tile_pool(name="staging", bufs=6))
        keep_ps = pools.enter_context(tc.psum_pool(name="keep_ps", bufs=1))
        turn_ps = pools.enter_context(tc.psum_pool(name="turn_ps", bufs=7))

        groups = [(batch, span) for span in range(SPANS) for batch in range(BATCH)]

        def load_x(g, x_rows, first=0, last=BLOCKS):
            batch, span = groups[g]
            rows = x[batch, span * TOKENS : (span + 1) * TOKENS, :].rearrange("(n p) k -> p n k", p=P)
            nc.sync.dma_start(out=x_rows[:, first:last, :], in_=rows[:, first:last, :])

        raw_words = const.tile([P, 2, 2 * FEAT], U8, align_bytes=64)
        raw_scales = const.tile([P, 2, FEAT], U8, align_bytes=64)
        nc.vector.memset(raw_scales[:].bitcast(I32), 0)
        loaded = {0: x_in.tile([P, BLOCKS, DIM], BF16, name="x_rows")}
        load_x(0, loaded[0], 0, BLOCKS // 2)
        for proj, scales in enumerate((Wq_scales, Wk_scales)):
            for quad in range(4):
                nc.sync.dma_start(
                    out=raw_scales[32 * quad : 32 * quad + 4, proj, :].bitcast(I32),
                    in_=scales[0, 4 * quad : 4 * quad + 4, :].bitcast(I32),
                )
        nc.sync.dma_start(out=raw_words[:, 0, :].bitcast(I32), in_=Wq_words[0].bitcast(I32))
        rows_each = FEAT // WIDE
        bias_rows = const.tile([P, WIDE], BF16)
        nc.vector.memset(bias_rows[:], 0.0)
        nc.sync.dma_start(out=bias_rows[0:rows_each, :], in_=bq.rearrange("(t p) -> t p", p=WIDE))
        nc.sync.dma_start(out=bias_rows[rows_each : 2 * rows_each, :], in_=bk.rearrange("(t p) -> t p", p=WIDE))
        load_x(0, loaded[0], BLOCKS // 2, BLOCKS)
        nc.sync.dma_start(out=raw_words[:, 1, :].bitcast(I32), in_=Wk_words[0].bitcast(I32))
        loaded[1] = x_in.tile([P, BLOCKS, DIM], BF16, name="x_rows")
        load_x(1, loaded[1])

        w_words = const.tile([P, 2, 2, FEAT], U8, align_bytes=64)
        w_scales = const.tile([P, 2, 2, HALF], U8, align_bytes=64)

        def part_weights(proj, h):
            for source in range(2):
                first = HALF * source + WIDE * h
                c = slice(first // 2, first // 2 + P)
                nc.vector.tensor_copy(
                    out=w_words[:, proj, :, 2 * c.start : 2 * c.stop].rearrange("p a (m b) -> p m a b", b=2),
                    in_=raw_words[:, proj, 2 * first : 2 * (first + WIDE)].rearrange(
                        "p (m a b) -> p m a b", a=2, b=2
                    ),
                )
                nc.vector.tensor_copy(
                    out=w_scales[:, proj, :, c].rearrange("p a m -> p m a"),
                    in_=raw_scales[:, proj, first : first + WIDE].rearrange("p (m a) -> p m a", a=2),
                )

        ident = const.tile([P, P], F32)
        make_identity(nc, ident[:])

        ratio = ROPE_BASE ** (-2.0 / FEAT)
        ratio_row = const.tile([P, P], F32)
        nc.vector.memset(ratio_row[:, 0:1], 1.0)
        width = 1
        while width < P:
            nc.vector.tensor_scalar_mul(
                out=ratio_row[:, width : 2 * width],
                in0=ratio_row[:, 0:width],
                scalar1=ratio**width,
            )
            width *= 2

        turned = keep_ps.tile([P, 3, P], F32)
        nc.tensor.transpose(turned[:, 2, :], ratio_row[:], ident[:])

        position = const.tile([P, SEQ], F32)
        nc.gpsimd.iota(
            position[:], pattern=[[1, SEQ]], base=0, channel_multiplier=0, allow_small_or_imprecise_dtypes=True
        )

        quarter = const.tile([P, 1], F32)
        nc.vector.memset(quarter[:], 0.25)
        quarter_turn = const.tile([P, 1], F32)
        nc.vector.tensor_scalar_mul(out=quarter_turn[:], in0=quarter[:], scalar1=2.0 * math.pi)

        turns = const.tile([P, TILES, 2], F32)
        for h in range(TILES):
            for j in range(2):
                first = ratio ** ((HALF * j + WIDE * h) // 2) / (2.0 * math.pi)
                nc.vector.tensor_scalar_mul(
                    out=turns[:, h, j : j + 1],
                    in0=turned[:, 2, 0:1],
                    scalar1=first if j == 1 else -first,
                )

        table = const.tile([P, TILES, 2, 2, SEQ], F32)

        def table_stage(first, width, h, stage_no, kept):
            cols = slice(first, first + width)
            kind, j = divmod(stage_no, 2)
            if stage_no == 0:
                whole = angle.tile([P, 2, width], I32)
                part = angle.tile([P, 2, width], F32)
                size = angle.tile([P, 2, width], F32)
                for half in range(2):
                    nc.vector.tensor_scalar_mul(
                        out=whole[:, half, :], in0=position[:, cols], scalar1=turns[:, h, half : half + 1]
                    )
                    nc.vector.scalar_tensor_tensor(
                        out=part[:, half, :],
                        in0=position[:, cols],
                        scalar=turns[:, h, half : half + 1],
                        in1=whole[:, half, :],
                        op0=ALU.mult,
                        op1=ALU.subtract,
                    )
                kept["part"] = part
                kept["size"] = size
            part, size = kept["part"], kept["size"]
            if kind == 0:
                nc.scalar.activation(
                    out=table[:, h, 1 - j, j, cols], in_=part[:, j, :], func=ACT.Sin, scale=2.0 * math.pi
                )
            if kind == 1:
                nc.scalar.activation(out=size[:, j, :], in_=part[:, j, :], func=ACT.Abs)
            if kind == 2:
                nc.scalar.activation(
                    out=table[:, h, j, j, cols],
                    in_=size[:, j, :],
                    func=ACT.Sin,
                    scale=-2.0 * math.pi,
                    bias=quarter_turn[:, 0:1],
                )

        def build_tables(first, width, h):
            kept = {}
            for stage_no in range(STAGES):
                table_stage(first, width, h, stage_no, kept)

        build_tables(0, EDGE_TOKENS, 0)

        bias_rows_f32 = const.tile([P, 2, P], F32)
        nc.vector.tensor_copy(out=bias_rows_f32[:], in_=bias_rows[:].rearrange("t (m a) -> t a m", a=2))
        for parity in range(2):
            nc.tensor.transpose(turned[:, parity, :], bias_rows_f32[:, parity, :], ident[:])
        bias = const.tile([P, 2 * rows_each], F32)
        nc.vector.tensor_copy(out=bias[:], in_=turned[:, 0, 0 : 2 * rows_each])

        def turn_x(x_rows, grouped, c):
            grouped_words = grouped[:].bitcast(F32).rearrange(
                "p (c n m u) -> p c n m u", c=BLOCKS // 2, n=2, u=2
            )
            planes = turn_ps.tile([P, 2, 2, P], F32, name="bank", tag="bank")
            for n in range(2):
                words = x_rows[:, 2 * c + n, :].bitcast(F32)
                for u in range(2):
                    nc.tensor.transpose(planes[:, n, u, :], words[:, u:WORDS:2], ident[:])
            nc.scalar.copy(out=grouped_words[:, c], in_=planes[:].rearrange("p n u m -> p n m u"))

        def quantise(grouped, codes, scales, some=slice(0, TOKENS)):
            nc.vector.quantize_mx(
                out=codes[:, some].bitcast(FP8X4),
                scales=scales[:, some],
                in_=grouped[:, 4 * some.start : 4 * some.stop],
            )

        def new_codes():
            codes = x_mx.tile([P, TOKENS], U32, align_bytes=64)
            scales = x_mx.tile([P, TOKENS], U8, align_bytes=64)
            return codes, scales

        def project(x_group, proj, h, parity, source, some):
            codes, scales = x_group
            bank = turn_ps.tile([P, TOKENS], F32, name="bank", tag="bank")
            c = (HALF * source + WIDE * h) // 2
            nc.tensor.matmul_mx(
                out=bank[:, 0 : some.stop - some.start],
                lhsT=w_words[:, proj, parity, 2 * c : 2 * (c + P)].bitcast(FP4X4),
                lhsT_scale=w_scales[:, proj, parity, c : c + P],
                rhs=codes[:, some].bitcast(FP8X4),
                rhs_scale=scales[:, some],
                start=True,
                stop=True,
            )
            return bank

        batches = [(0, proj, h) for h in range(TILES) for proj in range(2)]
        batches.extend(
            (g, proj, h) for g in range(1, len(groups)) for proj in range(2) for h in range(TILES)
        )
        per_group = 2 * TILES

        x_of = {}
        products_of = {}
        halves = {}
        later = {}

        def is_edge(m):
            return m == 0 or m == len(batches) - 1

        def front(m, some=slice(0, TOKENS)):
            g, proj, h = batches[m]
            width = some.stop - some.start
            cols = slice(groups[g][1] * TOKENS + some.start, groups[g][1] * TOKENS + some.stop)
            banks = {}
            for parity in range(2):
                for source in range(2):
                    banks[parity, source] = project(x_of[g], proj, h, parity, source, some)
            if some.start == 0:
                products_of[m] = rotated.tile([P, 2, 2, 2, TOKENS], F32, name="products")
            products = products_of[m]
            t = 2 * TILES * proj + h
            lower_sb = lifted.tile([P, TOKENS], F32)
            nc.scalar.activation(
                out=lower_sb[:, 0:width],
                in_=banks[0, 0][:, 0:width],
                func=ACT.Identity,
                bias=bias[:, t : t + 1],
                scale=1.0,
            )
            nc.gpsimd.tensor_tensor(
                out=products[:, 0, 0, :, some],
                in0=lower_sb[:, 0:width].unsqueeze(1).to_broadcast([P, 2, width]),
                in1=table[:, h, 0, :, cols],
                op=ALU.mult,
            )
            for parity, source in ((0, 1), (1, 0), (1, 1)):
                t = 2 * TILES * proj + TILES * source + h
                nc.vector.scalar_tensor_tensor(
                    out=products[:, parity, source, :, some],
                    in0=banks[parity, source][:, 0:width].unsqueeze(1).to_broadcast([P, 2, width]),
                    scalar=turned[:, parity, t : t + 1],
                    in1=table[:, h, source, :, cols],
                    op0=ALU.add,
                    op1=ALU.mult,
                )
            if not is_edge(m):
                nc.gpsimd.tensor_tensor(
                    out=products[:, 0, 0, 0, :],
                    in0=products[:, 0, 0, 0, :],
                    in1=products[:, 0, 1, 0, :],
                    op=ALU.add,
                )

        def back(m):
            g, proj, h = batches[m]
            batch, span = groups[g]
            products = products_of[m]
            rows = outs[proj][batch, span * TOKENS : (span + 1) * TOKENS, :]
            rows = rows.rearrange("(n p) i -> p n i", p=P)
            stages = [staging.tile([P, BLOCKS, WIDE], F32, name="stage") for j in range(2)]
            banks = [(j, c) for j in (1, 0) for c in range(2)]
            if is_edge(m):
                banks = [(j, c) for c in range(2) for j in (1, 0)]
            for j, c in banks:
                some = slice(2 * c, 2 * c + 2)
                sums = turn_ps.tile([P, 2, 2, P], F32, name="bank", tag="bank")
                for n in range(2):
                    first = (2 * c + n) * P
                    for parity in range(2):
                        terms = 1 if (j == 0 and parity == 0 and not is_edge(m)) else 2
                        for source in range(terms):
                            nc.tensor.matmul(
                                out=sums[:, n, parity, :],
                                lhsT=products[:, parity, source, j, first : first + P],
                                rhs=ident[:],
                                is_transpose=True,
                                start=(source == 0),
                                stop=(source == terms - 1),
                            )
                nc.scalar.copy(
                    out=stages[j][:, some, :].rearrange("p n (m a) -> p n m a", a=2),
                    in_=sums[:].rearrange("p n a m -> p n m a"),
                )
                new = slice(HALF * j + WIDE * h, HALF * j + WIDE * (h + 1))
                if is_edge(m):
                    nc.sync.dma_start(out=rows[:, some, new], in_=stages[j][:, some, :])
                elif c == 1:
                    nc.sync.dma_start(out=rows[:, :, new], in_=stages[j][:])

        part_weights(0, 0)
        grouped = x_mx.tile([P, 4 * TOKENS], BF16, align_bytes=64)
        x_of[0] = new_codes()
        for piece in range(EDGE_PIECES):
            some = slice(piece * EDGE_TOKENS, (piece + 1) * EDGE_TOKENS)
            turn_x(loaded[0], grouped, piece)
            quantise(grouped, *x_of[0], some)
            if piece > 0:
                build_tables(some.start, EDGE_TOKENS, 0)
            front(0, some)
        part_weights(1, 0)
        build_tables(0, TOKENS, 1)
        for m in range(len(batches)):
            g = batches[m][0]
            place = m % per_group
            if place == 0 and g + 2 < len(groups):
                loaded[g + 2] = x_in.tile([P, BLOCKS, DIM], BF16, name="x_rows")
                load_x(g + 2, loaded[g + 2])
            if m + 1 < len(batches):
                if is_edge(m + 1):
                    for piece in range(EDGE_PIECES):
                        front(m + 1, slice(piece * EDGE_TOKENS, (piece + 1) * EDGE_TOKENS))
                else:
                    front(m + 1)
            if g + 1 < len(groups):
                if place == 0:
                    halves[0] = x_mx.tile([P, 4 * TOKENS], BF16, align_bytes=64, name="grouped")
                if place < BLOCKS // 2:
                    turn_x(loaded[g + 1], halves[0], place)
                if place == BLOCKS // 2:
                    x_of[g + 1] = new_codes()
                    quantise(halves[0], *x_of[g + 1])
            if m < 2:
                part_weights(m, 1)
            if 3 <= m < 3 + TILES * STAGES:
                table_stage(TOKENS, TOKENS, (m - 3) // STAGES, (m - 3) % STAGES, later)
            back(m)
